import numpy as np
import ml_dtypes


def mxq(x, axis, fmt="e4m3"):
    dtype, down = {"e4m3": (ml_dtypes.float8_e4m3fn, 7), "e5m2": (ml_dtypes.float8_e5m2, 14)}[fmt]
    v = np.moveaxis(np.asarray(x, np.float32).astype(ml_dtypes.bfloat16).astype(np.float64), axis, -1)
    blocks = v.reshape(v.shape[:-1] + (-1, 32))
    amax = np.abs(blocks).max(-1, keepdims=True)
    byte = np.maximum(np.where(amax > 0, np.frexp(amax)[1] - 1 + 127, 0) - down, 1)
    scale = np.exp2(byte - 127.0)
    codes = (blocks / scale).astype(np.float32).astype(dtype).astype(np.float64)
    return np.moveaxis((codes * scale).reshape(v.shape), -1, axis)


WIDE = False


def mx_kscale(k):
    if not WIDE:
        return np.ones(k)
    levels = np.array([10, -10, 5, -5, 0])
    a = np.random.permutation(np.resize(levels, k // 512 * 4)).reshape(k // 512, 4)
    idx = np.arange(k)
    return np.exp2(a[idx // 512, idx % 128 // 32])


BF16 = ml_dtypes.bfloat16


def bf(x):
    return np.asarray(x, np.float32).astype(BF16)


def f64(x):
    return np.asarray(x).astype(np.float64)


N, D, K, R, ITERS = 4096, 512, 128, 3, 2
BETA = 5.0
NOISE = 0.7
KAPPA = 2.5


def softmax_rows(v):
    e = np.exp(v - v.max(axis=1, keepdims=True))
    return e / e.sum(axis=1, keepdims=True)


def unit_rows(v):
    return v / np.sqrt((v * v).sum(axis=1, keepdims=True))


def setup_inputs():
    t = mx_kscale(D)[::D // K]
    z = np.random.standard_normal((N, R))
    x = z @ np.random.standard_normal((R, D)) + NOISE * np.random.standard_normal((N, D))
    m = np.random.standard_normal((K, R))
    r = softmax_rows(KAPPA * (unit_rows(z) @ unit_rows(m).T) + 0.5 * np.random.standard_normal((N, K)))
    return {"x1": bf(x / np.sqrt(D * (R + NOISE * NOISE))), "r": bf(r * t[None, :])}


def reference(x1, r):
    x1, r = f64(x1), f64(r)
    xn = x1 / np.sqrt((x1 * x1).sum(axis=1, keepdims=True))
    cluster_r = r.sum(axis=0)
    mu = (mxq(r, 0, "e4m3").T @ mxq(xn, 0, "e4m3")) / cluster_r[:, None]
    r_new = softmax_rows(BETA * (mxq(xn, 1, "e4m3") @ mxq(mu, 1, "e4m3").T))
    return mu, r_new

@@ -1,0 +1,272 @@
+from contextlib import ExitStack
+
+import concourse.mybir as mybir
+from concourse.masks import make_identity
+
+F32 = mybir.dt.float32
+BF16 = mybir.dt.bfloat16
+U32 = mybir.dt.uint32
+U8 = mybir.dt.uint8
+FP8X4 = mybir.dt.float8_e4m3fn_x4
+ACT = mybir.ActivationFunctionType
+ALU = mybir.AluOpType
+AXIS = mybir.AxisListType
+
+ROWS = 4096
+D = 512
+K = 128
+BETA = 5.0
+P = 128
+PACK = 4
+PAIR = 2
+CHUNK = P * PACK
+CHUNKS = ROWS // CHUNK
+ONES_COLS = 32
+AHEAD = 3
+FEATURE_LEAD = 4
+
+FLOPS = 2 * 2 * ROWS * D * K
+
+
+def tile_clusternet_pb_kernel(tc, x1, r, out_0, out_1):
+    nc = tc.nc
+    x_chunks = x1.rearrange("(c p j) d -> c p j d", p=P, j=PACK)
+    r_halves = r.rearrange("(h c p j) k -> h p c (j k)", h=2, p=P, j=PACK)
+    r_new_chunks = out_1.rearrange("(c p j) k -> c p j k", p=P, j=PACK)
+    half_chunks = CHUNKS // 2
+
+    with ExitStack() as ctx:
+        ctx.enter_context(tc.manual_schedule())
+        keep = ctx.enter_context(tc.tile_pool(name="keep", bufs=1))
+        whole = ctx.enter_context(tc.tile_pool(name="whole", bufs=CHUNKS))
+        stream = ctx.enter_context(tc.tile_pool(name="stream", bufs=3))
+        small = ctx.enter_context(tc.tile_pool(name="small", bufs=4))
+        banks = ctx.enter_context(tc.psum_pool(name="banks", bufs=8))
+
+        r_raw = []
+        x_raw = []
+        for c in range(CHUNKS):
+            if c < 2:
+                r_half = keep.tile([P, half_chunks, PACK * K], BF16, name="r_half%d" % c)
+                nc.sync.dma_start(out=r_half[:], in_=r_halves[c])
+                r_raw.append(r_half)
+            x_chunk = whole.tile([P, PACK, D], BF16, name="x_chunk")
+            nc.sync.dma_start(out=x_chunk[:], in_=x_chunks[c])
+            x_raw.append(x_chunk)
+
+        ident = keep.tile([P, P], F32)
+        make_identity(nc, ident[:])
+        ones = keep.tile([P, ONES_COLS], BF16)
+        nc.vector.memset(ones[:], 1.0)
+        minus_half = keep.tile([P, PACK], F32)
+        nc.vector.memset(minus_half[:], -0.5)
+        warm = keep.tile([P, 1], F32)
+        nc.vector.memset(warm[:], 0.0)
+        nc.scalar.activation(out=warm[:], in_=warm[:], func=ACT.Exp)
+
+        colsum = banks.tile([P, ONES_COLS], F32, tag="bank")
+        r_codes = keep.tile([P, CHUNKS, K], U32, align_bytes=64)
+        r_scales = keep.tile([P, CHUNKS, K], U8, align_bytes=64)
+        for h in range(2):
+            r_by_row = r_raw[h][:].rearrange("p c (j k) -> p c j k", j=PACK)
+            for c in range(half_chunks):
+                for j in range(PACK):
+                    nc.tensor.matmul(
+                        out=colsum[:],
+                        lhsT=r_by_row[:, c, j, :],
+                        rhs=ones[:],
+                        start=(h == 0 and c == 0 and j == 0),
+                        stop=(h == 1 and c == half_chunks - 1 and j == PACK - 1),
+                    )
+            r_grouped = keep.tile([P, half_chunks, K, PACK], BF16, align_bytes=64, name="r_grouped%d" % h)
+            nc.vector.tensor_copy(out=r_grouped[:], in_=r_by_row.rearrange("p c j k -> p c k j"))
+            these = slice(h * half_chunks, (h + 1) * half_chunks)
+            nc.vector.quantize_mx(
+                out=r_codes[:, these, :].rearrange("p c k -> p (c k)").bitcast(FP8X4),
+                scales=r_scales[:, these, :].rearrange("p c k -> p (c k)"),
+                in_=r_grouped[:].rearrange("p c k j -> p (c k j)"),
+            )
+        inv_colsum = keep.tile([P, 1], F32)
+        nc.vector.reciprocal(inv_colsum[:], colsum[:, 0:1])
+
+        mu_sum = banks.tile([P, D], F32, tag="bank")
+        inv_norm = {}
+        xn = {}
+        xr_grouped = {}
+        flipped = {}
+        xf_grouped = {}
+        xf_codes = {}
+        xf_scales = {}
+
+        def square_rows(c):
+            sumsq = small.tile([P, PACK], F32)
+            for j in range(PACK):
+                squares = stream.tile([P, D], BF16)
+                nc.scalar.activation(
+                    out=squares[:],
+                    in_=x_raw[c][:, j, :],
+                    func=ACT.Square,
+                    accum_out=sumsq[:, j : j + 1],
+                )
+            inv_norm[c] = small.tile([P, PACK], F32, name="inv_norm")
+            nc.gpsimd.tensor_tensor(out=inv_norm[c][:], in0=sumsq[:], in1=minus_half[:], op=ALU.pow)
+
+        def scale_rows(c):
+            xn[c] = whole.tile([P, PACK, D], BF16, name="xn")
+            for j in range(PACK):
+                nc.vector.tensor_scalar_mul(
+                    out=xn[c][:, j, :], in0=x_raw[c][:, j, :], scalar1=inv_norm[c][:, j : j + 1]
+                )
+
+        def group_by_row(c):
+            xr_grouped[c] = stream.tile([P, D, PACK], BF16, align_bytes=64, name="xr_grouped")
+            nc.vector.tensor_copy(
+                out=xr_grouped[c][:].rearrange("p (g i) j -> p g j i", i=4),
+                in_=xn[c][:].rearrange("p j (g i) -> p g j i", i=4),
+            )
+
+        def first_matmul(c):
+            xr_codes = stream.tile([P, D], U32, align_bytes=64)
+            xr_scales = stream.tile([P, D], U8, align_bytes=64)
+            nc.vector.quantize_mx(
+                out=xr_codes[:].bitcast(FP8X4),
+                scales=xr_scales[:],
+                in_=xr_grouped[c][:].rearrange("p d j -> p (d j)"),
+            )
+            nc.tensor.matmul_mx(
+                out=mu_sum[:],
+                lhsT=r_codes[:, c, :].bitcast(FP8X4),
+                lhsT_scale=r_scales[:, c, :],
+                rhs=xr_codes[:].bitcast(FP8X4),
+                rhs_scale=xr_scales[:],
+                start=(c == 0),
+                stop=(c == CHUNKS - 1),
+            )
+
+        def transpose_rows(c):
+            words = xn[c][:].bitcast(F32)
+            flipped[c] = []
+            for half in range(2):
+                bank = banks.tile([P, 2, PAIR, P], F32, tag="bank")
+                for a in range(2):
+                    for u in range(PAIR):
+                        nc.tensor.transpose(
+                            bank[:, a, u, :], words[:, 2 * half + a, u * P : (u + 1) * P], ident[:]
+                        )
+                flipped[c].append(bank)
+
+        def empty_and_refill(c):
+            xf_grouped[c] = whole.tile([P, PACK, P, PACK], BF16, align_bytes=64, name="xf_grouped")
+            words = xf_grouped[c][:].bitcast(F32)
+            for half in range(2):
+                nc.scalar.copy(
+                    out=words[:, 2 * half : 2 * half + 2, :, :],
+                    in_=flipped[c][half][:].rearrange("p a u n -> p a n u"),
+                )
+            if c + AHEAD < CHUNKS:
+                transpose_rows(c + AHEAD)
+
+        def quantise_by_feature(c):
+            xf_codes[c] = whole.tile([P, PACK * P], U32, align_bytes=64, name="xf_codes")
+            xf_scales[c] = whole.tile([P, PACK * P], U8, align_bytes=64, name="xf_scales")
+            nc.vector.quantize_mx(
+                out=xf_codes[c][:].bitcast(FP8X4),
+                scales=xf_scales[c][:],
+                in_=xf_grouped[c][:].rearrange("p j n t -> p (j n t)"),
+            )
+
+        def stage(step, c):
+            if 0 <= c < CHUNKS:
+                step(c)
+
+        for t in range(CHUNKS + 2):
+            stage(square_rows, t)
+            stage(scale_rows, t - 1)
+            if t - 1 < AHEAD:
+                stage(transpose_rows, t - 1)
+            stage(empty_and_refill, t - CHUNKS)
+            stage(first_matmul, t - 2)
+            stage(group_by_row, t - 1)
+
+        quantise_by_feature(0)
+        mu_bf = keep.tile([P, D], BF16)
+        nc.vector.tensor_scalar_mul(out=mu_bf[:], in0=mu_sum[:], scalar1=inv_colsum[:, 0:1])
+        empty_and_refill(2)
+        quantise_by_feature(1)
+        mu_flipped = banks.tile([P, PAIR, K], F32, tag="bank")
+        for u in range(PAIR):
+            nc.tensor.transpose(
+                mu_flipped[:, u, :], mu_bf[:].bitcast(F32)[:, u * P : (u + 1) * P], ident[:]
+            )
+        mu_grouped = keep.tile([P, K, PACK], BF16, align_bytes=64)
+        nc.vector.tensor_copy(
+            out=mu_grouped[:].bitcast(F32), in_=mu_flipped[:].rearrange("p u k -> p k u")
+        )
+        empty_and_refill(3)
+        quantise_by_feature(2)
+        mu_codes = keep.tile([P, K], U32, align_bytes=64)
+        mu_scales = keep.tile([P, K], U8, align_bytes=64)
+        nc.vector.quantize_mx(
+            out=mu_codes[:].bitcast(FP8X4),
+            scales=mu_scales[:],
+            in_=mu_grouped[:].rearrange("p k t -> p (k t)"),
+        )
+        for c in range(4, CHUNKS):
+            empty_and_refill(c)
+        for c in range(3, FEATURE_LEAD):
+            quantise_by_feature(c)
+        mu = keep.tile([P, D], F32)
+        nc.scalar.activation(out=mu[:], in_=mu_sum[:], func=ACT.Copy, scale=inv_colsum[:, 0:1])
+        nc.sync.dma_start(out=out_0, in_=mu[:])
+
+        logits = {}
+        shift = {}
+        weights = {}
+        total = {}
+
+        def scores(c):
+            logits[c] = banks.tile([P, PACK, K], F32, tag="bank", name="logits")
+            for j in range(PACK):
+                nc.tensor.matmul_mx(
+                    out=logits[c][:, j, :],
+                    lhsT=xf_codes[c][:, j * P : (j + 1) * P].bitcast(FP8X4),
+                    lhsT_scale=xf_scales[c][:, j * P : (j + 1) * P],
+                    rhs=mu_codes[:].bitcast(FP8X4),
+                    rhs_scale=mu_scales[:],
+                    start=True,
+                    stop=True,
+                )
+            top = small.tile([P, PACK], F32)
+            nc.vector.tensor_reduce(out=top[:], in_=logits[c][:], axis=AXIS.X, op=ALU.max)
+            shift[c] = small.tile([P, PACK], F32, name="shift")
+            nc.vector.tensor_scalar_mul(out=shift[c][:], in0=top[:], scalar1=-BETA)
+
+        def exponentials(c):
+            weights[c] = stream.tile([P, PACK, K], F32, name="weights")
+            total[c] = small.tile([P, PACK], F32, name="total")
+            for j in range(PACK):
+                nc.scalar.activation(
+                    out=weights[c][:, j, :],
+                    in_=logits[c][:, j, :],
+                    func=ACT.Exp,
+                    bias=shift[c][:, j : j + 1],
+                    scale=BETA,
+                    accum_out=total[c][:, j : j + 1],
+                )
+
+        def divide_and_store(c):
+            inv_total = small.tile([P, PACK], F32)
+            nc.vector.reciprocal(inv_total[:], total[c][:])
+            nc.vector.tensor_tensor(
+                out=weights[c][:],
+                in0=weights[c][:],
+                in1=inv_total[:].unsqueeze(2).to_broadcast([P, PACK, K]),
+                op=ALU.mult,
+            )
+            nc.sync.dma_start(out=r_new_chunks[c], in_=weights[c][:])
+
+        for c in range(CHUNKS + 1):
+            stage(scores, c)
+            stage(quantise_by_feature, c + FEATURE_LEAD)
+            stage(exponentials, c)
+            stage(divide_and_store, c - 1)

@@ -41,6 +41,7 @@ def tile_clusternet_pb_kernel(tc, x1, r, out_0, out_1):
         whole = ctx.enter_context(tc.tile_pool(name="whole", bufs=CHUNKS))
         stream = ctx.enter_context(tc.tile_pool(name="stream", bufs=3))
         small = ctx.enter_context(tc.tile_pool(name="small", bufs=4))
+        results = ctx.enter_context(tc.tile_pool(name="results", bufs=4))
         banks = ctx.enter_context(tc.psum_pool(name="banks", bufs=8))
 
         r_raw = []
@@ -220,7 +221,7 @@ def tile_clusternet_pb_kernel(tc, x1, r, out_0, out_1):
         nc.sync.dma_start(out=out_0, in_=mu[:])
 
         logits = {}
-        shift = {}
+        top = {}
         weights = {}
         total = {}
 
@@ -236,20 +237,20 @@ def tile_clusternet_pb_kernel(tc, x1, r, out_0, out_1):
                     start=True,
                     stop=True,
                 )
-            top = small.tile([P, PACK], F32)
-            nc.vector.tensor_reduce(out=top[:], in_=logits[c][:], axis=AXIS.X, op=ALU.max)
-            shift[c] = small.tile([P, PACK], F32, name="shift")
-            nc.vector.tensor_scalar_mul(out=shift[c][:], in0=top[:], scalar1=-BETA)
+            top[c] = small.tile([P, PACK], F32, name="top")
+            nc.vector.tensor_reduce(out=top[c][:], in_=logits[c][:], axis=AXIS.X, op=ALU.max)
 
         def exponentials(c):
-            weights[c] = stream.tile([P, PACK, K], F32, name="weights")
+            shift = small.tile([P, PACK], F32)
+            nc.vector.tensor_scalar_mul(out=shift[:], in0=top[c][:], scalar1=-BETA)
+            weights[c] = results.tile([P, PACK, K], F32, name="weights")
             total[c] = small.tile([P, PACK], F32, name="total")
             for j in range(PACK):
                 nc.scalar.activation(
                     out=weights[c][:, j, :],
                     in_=logits[c][:, j, :],
                     func=ACT.Exp,
-                    bias=shift[c][:, j : j + 1],
+                    bias=shift[:, j : j + 1],
                     scale=BETA,
                     accum_out=total[c][:, j : j + 1],
                 )
@@ -257,7 +258,8 @@ def tile_clusternet_pb_kernel(tc, x1, r, out_0, out_1):
         def divide_and_store(c):
             inv_total = small.tile([P, PACK], F32)
             nc.vector.reciprocal(inv_total[:], total[c][:])
-            nc.vector.tensor_tensor(
+            divider = nc.gpsimd if c % 2 == 0 else nc.vector
+            divider.tensor_tensor(
                 out=weights[c][:],
                 in0=weights[c][:],
                 in1=inv_total[:].unsqueeze(2).to_broadcast([P, PACK, K]),
@@ -265,8 +267,8 @@ def tile_clusternet_pb_kernel(tc, x1, r, out_0, out_1):
             )
             nc.sync.dma_start(out=r_new_chunks[c], in_=weights[c][:])
 
-        for c in range(CHUNKS + 1):
+        for c in range(CHUNKS + 2):
             stage(scores, c)
+            stage(divide_and_store, c - 2)
             stage(quantise_by_feature, c + FEATURE_LEAD)
             stage(exponentials, c)
-            stage(divide_and_store, c - 1)

@@ -258,13 +258,21 @@ def tile_clusternet_pb_kernel(tc, x1, r, out_0, out_1):
         def divide_and_store(c):
             inv_total = small.tile([P, PACK], F32)
             nc.vector.reciprocal(inv_total[:], total[c][:])
-            divider = nc.gpsimd if c % 2 == 0 else nc.vector
-            divider.tensor_tensor(
-                out=weights[c][:],
-                in0=weights[c][:],
-                in1=inv_total[:].unsqueeze(2).to_broadcast([P, PACK, K]),
-                op=ALU.mult,
-            )
+            if c % 2 == 0:
+                nc.gpsimd.tensor_tensor(
+                    out=weights[c][:],
+                    in0=weights[c][:],
+                    in1=inv_total[:].unsqueeze(2).to_broadcast([P, PACK, K]),
+                    op=ALU.mult,
+                )
+            else:
+                for j in range(PACK):
+                    nc.scalar.activation(
+                        out=weights[c][:, j, :],
+                        in_=weights[c][:, j, :],
+                        func=ACT.Copy,
+                        scale=inv_total[:, j : j + 1],
+                    )
             nc.sync.dma_start(out=r_new_chunks[c], in_=weights[c][:])
 
         for c in range(CHUNKS + 2):

@@ -39,9 +39,9 @@ def tile_clusternet_pb_kernel(tc, x1, r, out_0, out_1):
         ctx.enter_context(tc.manual_schedule())
         keep = ctx.enter_context(tc.tile_pool(name="keep", bufs=1))
         whole = ctx.enter_context(tc.tile_pool(name="whole", bufs=CHUNKS))
-        stream = ctx.enter_context(tc.tile_pool(name="stream", bufs=3))
-        small = ctx.enter_context(tc.tile_pool(name="small", bufs=4))
-        results = ctx.enter_context(tc.tile_pool(name="results", bufs=4))
+        stream = ctx.enter_context(tc.tile_pool(name="stream", bufs=4))
+        small = ctx.enter_context(tc.tile_pool(name="small", bufs=CHUNKS))
+        results = ctx.enter_context(tc.tile_pool(name="results", bufs=CHUNKS))
         banks = ctx.enter_context(tc.psum_pool(name="banks", bufs=8))
 
         r_raw = []

@@ -59,11 +59,9 @@ def tile_clusternet_pb_kernel(tc, x1, r, out_0, out_1):
         make_identity(nc, ident[:])
         ones = keep.tile([P, ONES_COLS], BF16)
         nc.vector.memset(ones[:], 1.0)
-        minus_half = keep.tile([P, PACK], F32)
-        nc.vector.memset(minus_half[:], -0.5)
         warm = keep.tile([P, 1], F32)
-        nc.vector.memset(warm[:], 0.0)
-        nc.scalar.activation(out=warm[:], in_=warm[:], func=ACT.Exp)
+        nc.vector.memset(warm[:], 1.0)
+        nc.scalar.activation(out=warm[:], in_=warm[:], func=ACT.Abs_reciprocal_sqrt)
 
         colsum = banks.tile([P, ONES_COLS], F32, tag="bank")
         r_codes = keep.tile([P, CHUNKS, K], U32, align_bytes=64)
@@ -91,6 +89,7 @@ def tile_clusternet_pb_kernel(tc, x1, r, out_0, out_1):
         nc.vector.reciprocal(inv_colsum[:], colsum[:, 0:1])
 
         mu_sum = banks.tile([P, D], F32, tag="bank")
+        sumsq = {}
         inv_norm = {}
         xn = {}
         xr_grouped = {}
@@ -100,17 +99,24 @@ def tile_clusternet_pb_kernel(tc, x1, r, out_0, out_1):
         xf_scales = {}
 
         def square_rows(c):
-            sumsq = small.tile([P, PACK], F32)
+            if c < CHUNKS:
+                sumsq[c] = small.tile([P, PACK], F32, name="sumsq")
             for j in range(PACK):
+                if j == 1 or c == CHUNKS:
+                    stage(invert_norms, c - 1)
+                    if c == CHUNKS:
+                        return
                 squares = stream.tile([P, D], BF16)
                 nc.scalar.activation(
                     out=squares[:],
                     in_=x_raw[c][:, j, :],
                     func=ACT.Square,
-                    accum_out=sumsq[:, j : j + 1],
+                    accum_out=sumsq[c][:, j : j + 1],
                 )
+
+        def invert_norms(c):
             inv_norm[c] = small.tile([P, PACK], F32, name="inv_norm")
-            nc.gpsimd.tensor_tensor(out=inv_norm[c][:], in0=sumsq[:], in1=minus_half[:], op=ALU.pow)
+            nc.scalar.activation(out=inv_norm[c][:], in_=sumsq[c][:], func=ACT.Abs_reciprocal_sqrt)
 
         def scale_rows(c):
             xn[c] = whole.tile([P, PACK, D], BF16, name="xn")
@@ -181,7 +187,10 @@ def tile_clusternet_pb_kernel(tc, x1, r, out_0, out_1):
                 step(c)
 
         for t in range(CHUNKS + 2):
-            stage(square_rows, t)
+            if t <= CHUNKS:
+                square_rows(t)
+            if t == CHUNKS:
+                nc.scalar.activation(out=warm[:], in_=warm[:], func=ACT.Exp)
             stage(scale_rows, t - 1)
             if t - 1 < AHEAD:
                 stage(transpose_rows, t - 1)

@@ -21,19 +21,24 @@ PACK = 4
 PAIR = 2
 CHUNK = P * PACK
 CHUNKS = ROWS // CHUNK
+R_PARTS = 4
 ONES_COLS = 32
 AHEAD = 3
-FEATURE_LEAD = 4
+FEATURE_LEAD = 5
 
+DIVIDE_LAG = 2
+QFIRST = 1
+MU_AFTER = 0
+BY_GPSIMD = (0, 1, 3)
 FLOPS = 2 * 2 * ROWS * D * K
 
 
 def tile_clusternet_pb_kernel(tc, x1, r, out_0, out_1):
     nc = tc.nc
     x_chunks = x1.rearrange("(c p j) d -> c p j d", p=P, j=PACK)
-    r_halves = r.rearrange("(h c p j) k -> h p c (j k)", h=2, p=P, j=PACK)
+    r_parts = r.rearrange("(h c p j) k -> h p c (j k)", h=R_PARTS, p=P, j=PACK)
     r_new_chunks = out_1.rearrange("(c p j) k -> c p j k", p=P, j=PACK)
-    half_chunks = CHUNKS // 2
+    part_chunks = CHUNKS // R_PARTS
 
     with ExitStack() as ctx:
         ctx.enter_context(tc.manual_schedule())
@@ -46,14 +51,25 @@ def tile_clusternet_pb_kernel(tc, x1, r, out_0, out_1):
 
         r_raw = []
         x_raw = []
-        for c in range(CHUNKS):
-            if c < 2:
-                r_half = keep.tile([P, half_chunks, PACK * K], BF16, name="r_half%d" % c)
-                nc.sync.dma_start(out=r_half[:], in_=r_halves[c])
-                r_raw.append(r_half)
-            x_chunk = whole.tile([P, PACK, D], BF16, name="x_chunk")
-            nc.sync.dma_start(out=x_chunk[:], in_=x_chunks[c])
-            x_raw.append(x_chunk)
+        def load_r(h):
+            r_part = keep.tile([P, part_chunks, PACK * K], BF16, name="r_part%d" % h)
+            nc.sync.dma_start(out=r_part[:], in_=r_parts[h])
+            r_raw.append(r_part)
+
+        def load_x(c, rows):
+            if len(x_raw) == c:
+                x_raw.append(whole.tile([P, PACK, D], BF16, name="x_chunk"))
+            nc.sync.dma_start(out=x_raw[c][:, rows, :], in_=x_chunks[c][:, rows, :])
+
+        load_x(0, slice(0, 2))
+        load_r(0)
+        load_x(0, slice(2, PACK))
+        load_r(1)
+        load_r(2)
+        load_x(1, slice(0, PACK))
+        load_r(3)
+        for c in range(2, CHUNKS):
+            load_x(c, slice(0, PACK))
 
         ident = keep.tile([P, P], F32)
         make_identity(nc, ident[:])
@@ -66,27 +82,32 @@ def tile_clusternet_pb_kernel(tc, x1, r, out_0, out_1):
         colsum = banks.tile([P, ONES_COLS], F32, tag="bank")
         r_codes = keep.tile([P, CHUNKS, K], U32, align_bytes=64)
         r_scales = keep.tile([P, CHUNKS, K], U8, align_bytes=64)
-        for h in range(2):
+        r_grouped = {}
+
+        def group_r(h):
             r_by_row = r_raw[h][:].rearrange("p c (j k) -> p c j k", j=PACK)
-            for c in range(half_chunks):
+            for c in range(part_chunks):
                 for j in range(PACK):
                     nc.tensor.matmul(
                         out=colsum[:],
                         lhsT=r_by_row[:, c, j, :],
                         rhs=ones[:],
                         start=(h == 0 and c == 0 and j == 0),
-                        stop=(h == 1 and c == half_chunks - 1 and j == PACK - 1),
+                        stop=(h == R_PARTS - 1 and c == part_chunks - 1 and j == PACK - 1),
                     )
-            r_grouped = keep.tile([P, half_chunks, K, PACK], BF16, align_bytes=64, name="r_grouped%d" % h)
-            nc.vector.tensor_copy(out=r_grouped[:], in_=r_by_row.rearrange("p c j k -> p c k j"))
-            these = slice(h * half_chunks, (h + 1) * half_chunks)
+            r_grouped[h] = keep.tile([P, part_chunks, K, PACK], BF16, align_bytes=64, name="r_grouped%d" % h)
+            nc.vector.tensor_copy(
+                out=r_grouped[h][:].rearrange("p c (g i) j -> p c g j i", i=4),
+                in_=r_by_row.rearrange("p c j (g i) -> p c g j i", i=4),
+            )
+
+        def quantise_r(h):
+            these = slice(h * part_chunks, (h + 1) * part_chunks)
             nc.vector.quantize_mx(
                 out=r_codes[:, these, :].rearrange("p c k -> p (c k)").bitcast(FP8X4),
                 scales=r_scales[:, these, :].rearrange("p c k -> p (c k)"),
-                in_=r_grouped[:].rearrange("p c k j -> p (c k j)"),
+                in_=r_grouped[h][:].rearrange("p c k j -> p (c k j)"),
             )
-        inv_colsum = keep.tile([P, 1], F32)
-        nc.vector.reciprocal(inv_colsum[:], colsum[:, 0:1])
 
         mu_sum = banks.tile([P, D], F32, tag="bank")
         sumsq = {}
@@ -99,13 +120,10 @@ def tile_clusternet_pb_kernel(tc, x1, r, out_0, out_1):
         xf_scales = {}
 
         def square_rows(c):
-            if c < CHUNKS:
-                sumsq[c] = small.tile([P, PACK], F32, name="sumsq")
+            sumsq[c] = small.tile([P, PACK], F32, name="sumsq")
             for j in range(PACK):
-                if j == 1 or c == CHUNKS:
-                    stage(invert_norms, c - 1)
-                    if c == CHUNKS:
-                        return
+                if j == 1 and c > 2:
+                    invert_norms(c - 1)
                 squares = stream.tile([P, D], BF16)
                 nc.scalar.activation(
                     out=squares[:],
@@ -186,32 +204,53 @@ def tile_clusternet_pb_kernel(tc, x1, r, out_0, out_1):
             if 0 <= c < CHUNKS:
                 step(c)
 
-        for t in range(CHUNKS + 2):
-            if t <= CHUNKS:
-                square_rows(t)
-            if t == CHUNKS:
+        square_rows(0)
+        invert_norms(0)
+        group_r(0)
+        for h in range(1, R_PARTS - 1):
+            group_r(h)
+            quantise_r(h - 1)
+        for c in range(CHUNKS):
+            if c + 1 < CHUNKS:
+                square_rows(c + 1)
+                if c == 0:
+                    invert_norms(1)
+            else:
+                invert_norms(c)
                 nc.scalar.activation(out=warm[:], in_=warm[:], func=ACT.Exp)
-            stage(scale_rows, t - 1)
-            if t - 1 < AHEAD:
-                stage(transpose_rows, t - 1)
-            stage(empty_and_refill, t - CHUNKS)
-            stage(first_matmul, t - 2)
-            stage(group_by_row, t - 1)
+            scale_rows(c)
+            if c < AHEAD:
+                transpose_rows(c)
+            if c == 0:
+                quantise_r(R_PARTS - 2)
+            else:
+                first_matmul(c - 1)
+            group_by_row(c)
+            if c == 0:
+                group_r(R_PARTS - 1)
+            if c == 1:
+                quantise_r(R_PARTS - 1)
+        inv_colsum = keep.tile([P, 1], F32)
+        nc.vector.reciprocal(inv_colsum[:], colsum[:, 0:1])
+        empty_and_refill(0)
+        first_matmul(CHUNKS - 1)
+        empty_and_refill(1)
 
         quantise_by_feature(0)
-        mu_bf = keep.tile([P, D], BF16)
-        nc.vector.tensor_scalar_mul(out=mu_bf[:], in0=mu_sum[:], scalar1=inv_colsum[:, 0:1])
-        empty_and_refill(2)
+        mu = keep.tile([P, D], F32)
+        nc.vector.tensor_scalar_mul(out=mu[:], in0=mu_sum[:], scalar1=inv_colsum[:, 0:1])
+        nc.sync.dma_start(out=out_0, in_=mu[:])
         quantise_by_feature(1)
-        mu_flipped = banks.tile([P, PAIR, K], F32, tag="bank")
+        mu_flipped = banks.tile([P, PACK, K], F32, tag="bank")
+        mu_words = mu[:].rearrange("p (u q e) -> p u q e", u=PAIR, e=PAIR)
         for u in range(PAIR):
-            nc.tensor.transpose(
-                mu_flipped[:, u, :], mu_bf[:].bitcast(F32)[:, u * P : (u + 1) * P], ident[:]
-            )
+            for e in range(PAIR):
+                nc.tensor.transpose(mu_flipped[:, PAIR * u + e, :], mu_words[:, u, :, e], ident[:])
         mu_grouped = keep.tile([P, K, PACK], BF16, align_bytes=64)
         nc.vector.tensor_copy(
-            out=mu_grouped[:].bitcast(F32), in_=mu_flipped[:].rearrange("p u k -> p k u")
+            out=mu_grouped[:], in_=mu_flipped[:].rearrange("p t k -> p k t")
         )
+        empty_and_refill(2)
         empty_and_refill(3)
         quantise_by_feature(2)
         mu_codes = keep.tile([P, K], U32, align_bytes=64)
@@ -225,14 +264,13 @@ def tile_clusternet_pb_kernel(tc, x1, r, out_0, out_1):
             empty_and_refill(c)
         for c in range(3, FEATURE_LEAD):
             quantise_by_feature(c)
-        mu = keep.tile([P, D], F32)
-        nc.scalar.activation(out=mu[:], in_=mu_sum[:], func=ACT.Copy, scale=inv_colsum[:, 0:1])
-        nc.sync.dma_start(out=out_0, in_=mu[:])
 
         logits = {}
         top = {}
         weights = {}
         total = {}
+        shift = {}
+        inv_total = {}
 
         def scores(c):
             logits[c] = banks.tile([P, PACK, K], F32, tag="bank", name="logits")
@@ -249,9 +287,11 @@ def tile_clusternet_pb_kernel(tc, x1, r, out_0, out_1):
             top[c] = small.tile([P, PACK], F32, name="top")
             nc.vector.tensor_reduce(out=top[c][:], in_=logits[c][:], axis=AXIS.X, op=ALU.max)
 
+        def shift_rows(c):
+            shift[c] = small.tile([P, PACK], F32, name="shift")
+            nc.vector.tensor_scalar_mul(out=shift[c][:], in0=top[c][:], scalar1=-BETA)
+
         def exponentials(c):
-            shift = small.tile([P, PACK], F32)
-            nc.vector.tensor_scalar_mul(out=shift[:], in0=top[c][:], scalar1=-BETA)
             weights[c] = results.tile([P, PACK, K], F32, name="weights")
             total[c] = small.tile([P, PACK], F32, name="total")
             for j in range(PACK):
@@ -259,33 +299,39 @@ def tile_clusternet_pb_kernel(tc, x1, r, out_0, out_1):
                     out=weights[c][:, j, :],
                     in_=logits[c][:, j, :],
                     func=ACT.Exp,
-                    bias=shift[:, j : j + 1],
+                    bias=shift[c][:, j : j + 1],
                     scale=BETA,
                     accum_out=total[c][:, j : j + 1],
                 )
 
+        def invert_totals(c):
+            inv_total[c] = small.tile([P, PACK], F32, name="inv_total")
+            nc.vector.reciprocal(inv_total[c][:], total[c][:])
+
         def divide_and_store(c):
-            inv_total = small.tile([P, PACK], F32)
-            nc.vector.reciprocal(inv_total[:], total[c][:])
-            if c % 2 == 0:
+            if c in BY_GPSIMD:
                 nc.gpsimd.tensor_tensor(
                     out=weights[c][:],
                     in0=weights[c][:],
-                    in1=inv_total[:].unsqueeze(2).to_broadcast([P, PACK, K]),
+                    in1=inv_total[c][:].unsqueeze(2).to_broadcast([P, PACK, K]),
                     op=ALU.mult,
                 )
             else:
                 for j in range(PACK):
-                    nc.scalar.activation(
+                    nc.vector.tensor_scalar_mul(
                         out=weights[c][:, j, :],
-                        in_=weights[c][:, j, :],
-                        func=ACT.Copy,
-                        scale=inv_total[:, j : j + 1],
+                        in0=weights[c][:, j, :],
+                        scalar1=inv_total[c][:, j : j + 1],
                     )
             nc.sync.dma_start(out=r_new_chunks[c], in_=weights[c][:])
 
-        for c in range(CHUNKS + 2):
+        for c in range(CHUNKS + DIVIDE_LAG):
             stage(scores, c)
-            stage(divide_and_store, c - 2)
-            stage(quantise_by_feature, c + FEATURE_LEAD)
+            if QFIRST:
+                stage(quantise_by_feature, c + FEATURE_LEAD)
+            stage(invert_totals, c - DIVIDE_LAG)
+            stage(shift_rows, c)
+            if not QFIRST:
+                stage(quantise_by_feature, c + FEATURE_LEAD)
+            stage(divide_and_store, c - DIVIDE_LAG)
             stage(exponentials, c)

@@ -24,12 +24,17 @@ CHUNKS = ROWS // CHUNK
 R_PARTS = 4
 ONES_COLS = 32
 AHEAD = 3
-FEATURE_LEAD = 5
+FEATURE_LEAD = 6
 
 DIVIDE_LAG = 2
+LOADS = "x0a r0 x0b r1 r2 x1 r3"
+TAIL = 1
+SC_EARLY = 0
+R_LATE = 1
 QFIRST = 1
 MU_AFTER = 0
-BY_GPSIMD = (0, 1, 3)
+BY_GPSIMD = ()
+BY_SCALAR = (1, 3)
 FLOPS = 2 * 2 * ROWS * D * K
 
 
@@ -61,13 +66,12 @@ def tile_clusternet_pb_kernel(tc, x1, r, out_0, out_1):
                 x_raw.append(whole.tile([P, PACK, D], BF16, name="x_chunk"))
             nc.sync.dma_start(out=x_raw[c][:, rows, :], in_=x_chunks[c][:, rows, :])
 
-        load_x(0, slice(0, 2))
-        load_r(0)
-        load_x(0, slice(2, PACK))
-        load_r(1)
-        load_r(2)
-        load_x(1, slice(0, PACK))
-        load_r(3)
+        pieces = {"": slice(0, PACK), "a": slice(0, 2), "b": slice(2, PACK), "i": slice(0, 1), "j": slice(1, 2)}
+        for it in LOADS.split(" "):
+            if it.startswith("r"):
+                load_r(int(it[1:]))
+            else:
+                load_x(int(it[1]), pieces[it[2:]])
         for c in range(2, CHUNKS):
             load_x(c, slice(0, PACK))
 
@@ -96,10 +100,7 @@ def tile_clusternet_pb_kernel(tc, x1, r, out_0, out_1):
                         stop=(h == R_PARTS - 1 and c == part_chunks - 1 and j == PACK - 1),
                     )
             r_grouped[h] = keep.tile([P, part_chunks, K, PACK], BF16, align_bytes=64, name="r_grouped%d" % h)
-            nc.vector.tensor_copy(
-                out=r_grouped[h][:].rearrange("p c (g i) j -> p c g j i", i=4),
-                in_=r_by_row.rearrange("p c j (g i) -> p c g j i", i=4),
-            )
+            nc.vector.tensor_copy(out=r_grouped[h][:], in_=r_by_row.rearrange("p c j k -> p c k j"))
 
         def quantise_r(h):
             these = slice(h * part_chunks, (h + 1) * part_chunks)
@@ -237,18 +238,17 @@ def tile_clusternet_pb_kernel(tc, x1, r, out_0, out_1):
         empty_and_refill(1)
 
         quantise_by_feature(0)
-        mu = keep.tile([P, D], F32)
-        nc.vector.tensor_scalar_mul(out=mu[:], in0=mu_sum[:], scalar1=inv_colsum[:, 0:1])
-        nc.sync.dma_start(out=out_0, in_=mu[:])
+        mu_bf = keep.tile([P, D], BF16)
+        nc.vector.tensor_scalar_mul(out=mu_bf[:], in0=mu_sum[:], scalar1=inv_colsum[:, 0:1])
         quantise_by_feature(1)
-        mu_flipped = banks.tile([P, PACK, K], F32, tag="bank")
-        mu_words = mu[:].rearrange("p (u q e) -> p u q e", u=PAIR, e=PAIR)
+        mu_flipped = banks.tile([P, PAIR, K], F32, tag="bank")
         for u in range(PAIR):
-            for e in range(PAIR):
-                nc.tensor.transpose(mu_flipped[:, PAIR * u + e, :], mu_words[:, u, :, e], ident[:])
+            nc.tensor.transpose(
+                mu_flipped[:, u, :], mu_bf[:].bitcast(F32)[:, u * P : (u + 1) * P], ident[:]
+            )
         mu_grouped = keep.tile([P, K, PACK], BF16, align_bytes=64)
         nc.vector.tensor_copy(
-            out=mu_grouped[:], in_=mu_flipped[:].rearrange("p t k -> p k t")
+            out=mu_grouped[:].bitcast(F32), in_=mu_flipped[:].rearrange("p u k -> p k u")
         )
         empty_and_refill(2)
         empty_and_refill(3)
@@ -264,6 +264,11 @@ def tile_clusternet_pb_kernel(tc, x1, r, out_0, out_1):
             empty_and_refill(c)
         for c in range(3, FEATURE_LEAD):
             quantise_by_feature(c)
+
+        def store_mu():
+            mu = keep.tile([P, D], F32, name="mu")
+            nc.scalar.activation(out=mu[:], in_=mu_sum[:], func=ACT.Copy, scale=inv_colsum[:, 0:1])
+            nc.sync.dma_start(out=out_0, in_=mu[:])
 
         logits = {}
         top = {}
@@ -306,24 +311,30 @@ def tile_clusternet_pb_kernel(tc, x1, r, out_0, out_1):
 
         def invert_totals(c):
             inv_total[c] = small.tile([P, PACK], F32, name="inv_total")
-            nc.vector.reciprocal(inv_total[c][:], total[c][:])
+            if not (TAIL and c == CHUNKS - 1):
+                nc.vector.reciprocal(inv_total[c][:], total[c][:])
 
         def divide_and_store(c):
-            if c in BY_GPSIMD:
-                nc.gpsimd.tensor_tensor(
-                    out=weights[c][:],
-                    in0=weights[c][:],
-                    in1=inv_total[c][:].unsqueeze(2).to_broadcast([P, PACK, K]),
-                    op=ALU.mult,
-                )
-            else:
-                for j in range(PACK):
-                    nc.vector.tensor_scalar_mul(
-                        out=weights[c][:, j, :],
-                        in0=weights[c][:, j, :],
-                        scalar1=inv_total[c][:, j : j + 1],
-                    )
-            nc.sync.dma_start(out=r_new_chunks[c], in_=weights[c][:])
+            step = PACK // 2 if TAIL and c == CHUNKS - 1 else PACK
+            for first in range(0, PACK, step):
+                rows = slice(first, first + step)
+                if step < PACK:
+                    nc.vector.reciprocal(inv_total[c][:, rows], total[c][:, rows])
+                for j in range(first, first + step):
+                    if c in BY_SCALAR:
+                        nc.scalar.activation(
+                            out=weights[c][:, j, :],
+                            in_=weights[c][:, j, :],
+                            func=ACT.Copy,
+                            scale=inv_total[c][:, j : j + 1],
+                        )
+                    else:
+                        nc.vector.tensor_scalar_mul(
+                            out=weights[c][:, j, :],
+                            in0=weights[c][:, j, :],
+                            scalar1=inv_total[c][:, j : j + 1],
+                        )
+                nc.sync.dma_start(out=r_new_chunks[c][:, rows, :], in_=weights[c][:, rows, :])
 
         for c in range(CHUNKS + DIVIDE_LAG):
             stage(scores, c)
@@ -335,3 +346,5 @@ def tile_clusternet_pb_kernel(tc, x1, r, out_0, out_1):
                 stage(quantise_by_feature, c + FEATURE_LEAD)
             stage(divide_and_store, c - DIVIDE_LAG)
             stage(exponentials, c)
+            if c == MU_AFTER:
+                store_mu()

@@ -21,13 +21,15 @@ PACK = 4
 PAIR = 2
 CHUNK = P * PACK
 CHUNKS = ROWS // CHUNK
-R_PARTS = 4
+R_WIDTHS = (1, 1, 2, 2, 2)
+R_PARTS = len(R_WIDTHS)
 ONES_COLS = 32
 AHEAD = 3
 FEATURE_LEAD = 6
 
 DIVIDE_LAG = 2
-LOADS = "x0a r0 x0b r1 r2 x1 r3"
+LOADS = "r0 x0a r1 r2 x0b r3 x1a r4 x1b"
+R_FIRST = 4
 TAIL = 1
 SC_EARLY = 0
 R_LATE = 1
@@ -41,9 +43,9 @@ FLOPS = 2 * 2 * ROWS * D * K
 def tile_clusternet_pb_kernel(tc, x1, r, out_0, out_1):
     nc = tc.nc
     x_chunks = x1.rearrange("(c p j) d -> c p j d", p=P, j=PACK)
-    r_parts = r.rearrange("(h c p j) k -> h p c (j k)", h=R_PARTS, p=P, j=PACK)
+    r_chunks = r.rearrange("(c p j) k -> p c (j k)", p=P, j=PACK)
     r_new_chunks = out_1.rearrange("(c p j) k -> c p j k", p=P, j=PACK)
-    part_chunks = CHUNKS // R_PARTS
+    r_start = [sum(R_WIDTHS[:h]) for h in range(R_PARTS + 1)]
 
     with ExitStack() as ctx:
         ctx.enter_context(tc.manual_schedule())
@@ -57,8 +59,8 @@ def tile_clusternet_pb_kernel(tc, x1, r, out_0, out_1):
         r_raw = []
         x_raw = []
         def load_r(h):
-            r_part = keep.tile([P, part_chunks, PACK * K], BF16, name="r_part%d" % h)
-            nc.sync.dma_start(out=r_part[:], in_=r_parts[h])
+            r_part = keep.tile([P, R_WIDTHS[h], PACK * K], BF16, name="r_part%d" % h)
+            nc.sync.dma_start(out=r_part[:], in_=r_chunks[:, r_start[h] : r_start[h + 1], :])
             r_raw.append(r_part)
 
         def load_x(c, rows):
@@ -90,20 +92,20 @@ def tile_clusternet_pb_kernel(tc, x1, r, out_0, out_1):
 
         def group_r(h):
             r_by_row = r_raw[h][:].rearrange("p c (j k) -> p c j k", j=PACK)
-            for c in range(part_chunks):
+            for c in range(R_WIDTHS[h]):
                 for j in range(PACK):
                     nc.tensor.matmul(
                         out=colsum[:],
                         lhsT=r_by_row[:, c, j, :],
                         rhs=ones[:],
                         start=(h == 0 and c == 0 and j == 0),
-                        stop=(h == R_PARTS - 1 and c == part_chunks - 1 and j == PACK - 1),
+                        stop=(h == R_PARTS - 1 and c == R_WIDTHS[h] - 1 and j == PACK - 1),
                     )
-            r_grouped[h] = keep.tile([P, part_chunks, K, PACK], BF16, align_bytes=64, name="r_grouped%d" % h)
+            r_grouped[h] = keep.tile([P, R_WIDTHS[h], K, PACK], BF16, align_bytes=64, name="r_grouped%d" % h)
             nc.vector.tensor_copy(out=r_grouped[h][:], in_=r_by_row.rearrange("p c j k -> p c k j"))
 
         def quantise_r(h):
-            these = slice(h * part_chunks, (h + 1) * part_chunks)
+            these = slice(r_start[h], r_start[h + 1])
             nc.vector.quantize_mx(
                 out=r_codes[:, these, :].rearrange("p c k -> p (c k)").bitcast(FP8X4),
                 scales=r_scales[:, these, :].rearrange("p c k -> p (c k)"),
@@ -207,10 +209,9 @@ def tile_clusternet_pb_kernel(tc, x1, r, out_0, out_1):
 
         square_rows(0)
         invert_norms(0)
-        group_r(0)
-        for h in range(1, R_PARTS - 1):
+        for h in range(R_FIRST):
             group_r(h)
-            quantise_r(h - 1)
+            quantise_r(h)
         for c in range(CHUNKS):
             if c + 1 < CHUNKS:
                 square_rows(c + 1)
@@ -222,15 +223,13 @@ def tile_clusternet_pb_kernel(tc, x1, r, out_0, out_1):
             scale_rows(c)
             if c < AHEAD:
                 transpose_rows(c)
-            if c == 0:
-                quantise_r(R_PARTS - 2)
-            else:
+            if 0 < c < R_PARTS - R_FIRST + 1:
+                quantise_r(R_FIRST + c - 1)
+            if c < R_PARTS - R_FIRST:
+                group_r(R_FIRST + c)
+            if c > 0:
                 first_matmul(c - 1)
             group_by_row(c)
-            if c == 0:
-                group_r(R_PARTS - 1)
-            if c == 1:
-                quantise_r(R_PARTS - 1)
         inv_colsum = keep.tile([P, 1], F32)
         nc.vector.reciprocal(inv_colsum[:], colsum[:, 0:1])
         empty_and_refill(0)

from contextlib import ExitStack

import concourse.mybir as mybir
from concourse.masks import make_identity

F32 = mybir.dt.float32
BF16 = mybir.dt.bfloat16
U32 = mybir.dt.uint32
U8 = mybir.dt.uint8
FP8X4 = mybir.dt.float8_e4m3fn_x4
ACT = mybir.ActivationFunctionType
ALU = mybir.AluOpType
AXIS = mybir.AxisListType

ROWS = 4096
D = 512
K = 128
BETA = 5.0
P = 128
PACK = 4
PAIR = 2
CHUNK = P * PACK
CHUNKS = ROWS // CHUNK
R_WIDTHS = (1, 1, 2, 2, 2)
R_PARTS = len(R_WIDTHS)
ONES_COLS = 32
AHEAD = 3
FEATURE_LEAD = 6

DIVIDE_LAG = 2
LOADS = "r0 x0a r1 r2 x0b r3 x1a r4 x1b"
R_FIRST = 4
TAIL = 1
SC_EARLY = 0
R_LATE = 1
QFIRST = 1
MU_AFTER = 0
BY_GPSIMD = ()
BY_SCALAR = (1, 3)
FLOPS = 2 * 2 * ROWS * D * K


def tile_clusternet_pb_kernel(tc, x1, r, out_0, out_1):
    nc = tc.nc
    x_chunks = x1.rearrange("(c p j) d -> c p j d", p=P, j=PACK)
    r_chunks = r.rearrange("(c p j) k -> p c (j k)", p=P, j=PACK)
    r_new_chunks = out_1.rearrange("(c p j) k -> c p j k", p=P, j=PACK)
    r_start = [sum(R_WIDTHS[:h]) for h in range(R_PARTS + 1)]

    with ExitStack() as ctx:
        ctx.enter_context(tc.manual_schedule())
        keep = ctx.enter_context(tc.tile_pool(name="keep", bufs=1))
        whole = ctx.enter_context(tc.tile_pool(name="whole", bufs=CHUNKS))
        stream = ctx.enter_context(tc.tile_pool(name="stream", bufs=4))
        small = ctx.enter_context(tc.tile_pool(name="small", bufs=CHUNKS))
        results = ctx.enter_context(tc.tile_pool(name="results", bufs=CHUNKS))
        banks = ctx.enter_context(tc.psum_pool(name="banks", bufs=8))

        r_raw = []
        x_raw = []
        def load_r(h):
            r_part = keep.tile([P, R_WIDTHS[h], PACK * K], BF16, name="r_part%d" % h)
            nc.sync.dma_start(out=r_part[:], in_=r_chunks[:, r_start[h] : r_start[h + 1], :])
            r_raw.append(r_part)

        def load_x(c, rows):
            if len(x_raw) == c:
                x_raw.append(whole.tile([P, PACK, D], BF16, name="x_chunk"))
            nc.sync.dma_start(out=x_raw[c][:, rows, :], in_=x_chunks[c][:, rows, :])

        pieces = {"": slice(0, PACK), "a": slice(0, 2), "b": slice(2, PACK), "i": slice(0, 1), "j": slice(1, 2)}
        for it in LOADS.split(" "):
            if it.startswith("r"):
                load_r(int(it[1:]))
            else:
                load_x(int(it[1]), pieces[it[2:]])
        for c in range(2, CHUNKS):
            load_x(c, slice(0, PACK))

        ident = keep.tile([P, P], F32)
        make_identity(nc, ident[:])
        ones = keep.tile([P, ONES_COLS], BF16)
        nc.vector.memset(ones[:], 1.0)
        warm = keep.tile([P, 1], F32)
        nc.vector.memset(warm[:], 1.0)
        nc.scalar.activation(out=warm[:], in_=warm[:], func=ACT.Abs_reciprocal_sqrt)

        colsum = banks.tile([P, ONES_COLS], F32, tag="bank")
        r_codes = keep.tile([P, CHUNKS, K], U32, align_bytes=64)
        r_scales = keep.tile([P, CHUNKS, K], U8, align_bytes=64)
        r_grouped = {}

        def group_r(h):
            r_by_row = r_raw[h][:].rearrange("p c (j k) -> p c j k", j=PACK)
            for c in range(R_WIDTHS[h]):
                for j in range(PACK):
                    nc.tensor.matmul(
                        out=colsum[:],
                        lhsT=r_by_row[:, c, j, :],
                        rhs=ones[:],
                        start=(h == 0 and c == 0 and j == 0),
                        stop=(h == R_PARTS - 1 and c == R_WIDTHS[h] - 1 and j == PACK - 1),
                    )
            r_grouped[h] = keep.tile([P, R_WIDTHS[h], K, PACK], BF16, align_bytes=64, name="r_grouped%d" % h)
            nc.vector.tensor_copy(out=r_grouped[h][:], in_=r_by_row.rearrange("p c j k -> p c k j"))

        def quantise_r(h):
            these = slice(r_start[h], r_start[h + 1])
            nc.vector.quantize_mx(
                out=r_codes[:, these, :].rearrange("p c k -> p (c k)").bitcast(FP8X4),
                scales=r_scales[:, these, :].rearrange("p c k -> p (c k)"),
                in_=r_grouped[h][:].rearrange("p c k j -> p (c k j)"),
            )

        mu_sum = banks.tile([P, D], F32, tag="bank")
        sumsq = {}
        inv_norm = {}
        xn = {}
        xr_grouped = {}
        flipped = {}
        xf_grouped = {}
        xf_codes = {}
        xf_scales = {}

        def square_rows(c):
            sumsq[c] = small.tile([P, PACK], F32, name="sumsq")
            for j in range(PACK):
                if j == 1 and c > 2:
                    invert_norms(c - 1)
                squares = stream.tile([P, D], BF16)
                nc.scalar.activation(
                    out=squares[:],
                    in_=x_raw[c][:, j, :],
                    func=ACT.Square,
                    accum_out=sumsq[c][:, j : j + 1],
                )

        def invert_norms(c):
            inv_norm[c] = small.tile([P, PACK], F32, name="inv_norm")
            nc.scalar.activation(out=inv_norm[c][:], in_=sumsq[c][:], func=ACT.Abs_reciprocal_sqrt)

        def scale_rows(c):
            xn[c] = whole.tile([P, PACK, D], BF16, name="xn")
            for j in range(PACK):
                nc.vector.tensor_scalar_mul(
                    out=xn[c][:, j, :], in0=x_raw[c][:, j, :], scalar1=inv_norm[c][:, j : j + 1]
                )

        def group_by_row(c):
            xr_grouped[c] = stream.tile([P, D, PACK], BF16, align_bytes=64, name="xr_grouped")
            nc.vector.tensor_copy(
                out=xr_grouped[c][:].rearrange("p (g i) j -> p g j i", i=4),
                in_=xn[c][:].rearrange("p j (g i) -> p g j i", i=4),
            )

        def first_matmul(c):
            xr_codes = stream.tile([P, D], U32, align_bytes=64)
            xr_scales = stream.tile([P, D], U8, align_bytes=64)
            nc.vector.quantize_mx(
                out=xr_codes[:].bitcast(FP8X4),
                scales=xr_scales[:],
                in_=xr_grouped[c][:].rearrange("p d j -> p (d j)"),
            )
            nc.tensor.matmul_mx(
                out=mu_sum[:],
                lhsT=r_codes[:, c, :].bitcast(FP8X4),
                lhsT_scale=r_scales[:, c, :],
                rhs=xr_codes[:].bitcast(FP8X4),
                rhs_scale=xr_scales[:],
                start=(c == 0),
                stop=(c == CHUNKS - 1),
            )

        def transpose_rows(c):
            words = xn[c][:].bitcast(F32)
            flipped[c] = []
            for half in range(2):
                bank = banks.tile([P, 2, PAIR, P], F32, tag="bank")
                for a in range(2):
                    for u in range(PAIR):
                        nc.tensor.transpose(
                            bank[:, a, u, :], words[:, 2 * half + a, u * P : (u + 1) * P], ident[:]
                        )
                flipped[c].append(bank)

        def empty_and_refill(c):
            xf_grouped[c] = whole.tile([P, PACK, P, PACK], BF16, align_bytes=64, name="xf_grouped")
            words = xf_grouped[c][:].bitcast(F32)
            for half in range(2):
                nc.scalar.copy(
                    out=words[:, 2 * half : 2 * half + 2, :, :],
                    in_=flipped[c][half][:].rearrange("p a u n -> p a n u"),
                )
            if c + AHEAD < CHUNKS:
                transpose_rows(c + AHEAD)

        def quantise_by_feature(c):
            xf_codes[c] = whole.tile([P, PACK * P], U32, align_bytes=64, name="xf_codes")
            xf_scales[c] = whole.tile([P, PACK * P], U8, align_bytes=64, name="xf_scales")
            nc.vector.quantize_mx(
                out=xf_codes[c][:].bitcast(FP8X4),
                scales=xf_scales[c][:],
                in_=xf_grouped[c][:].rearrange("p j n t -> p (j n t)"),
            )

        def stage(step, c):
            if 0 <= c < CHUNKS:
                step(c)

        square_rows(0)
        invert_norms(0)
        for h in range(R_FIRST):
            group_r(h)
            quantise_r(h)
        for c in range(CHUNKS):
            if c + 1 < CHUNKS:
                square_rows(c + 1)
                if c == 0:
                    invert_norms(1)
            else:
                invert_norms(c)
                nc.scalar.activation(out=warm[:], in_=warm[:], func=ACT.Exp)
            scale_rows(c)
            if c < AHEAD:
                transpose_rows(c)
            if 0 < c < R_PARTS - R_FIRST + 1:
                quantise_r(R_FIRST + c - 1)
            if c < R_PARTS - R_FIRST:
                group_r(R_FIRST + c)
            if c > 0:
                first_matmul(c - 1)
            group_by_row(c)
        inv_colsum = keep.tile([P, 1], F32)
        nc.vector.reciprocal(inv_colsum[:], colsum[:, 0:1])
        empty_and_refill(0)
        first_matmul(CHUNKS - 1)
        empty_and_refill(1)

        quantise_by_feature(0)
        mu_bf = keep.tile([P, D], BF16)
        nc.vector.tensor_scalar_mul(out=mu_bf[:], in0=mu_sum[:], scalar1=inv_colsum[:, 0:1])
        quantise_by_feature(1)
        mu_flipped = banks.tile([P, PAIR, K], F32, tag="bank")
        for u in range(PAIR):
            nc.tensor.transpose(
                mu_flipped[:, u, :], mu_bf[:].bitcast(F32)[:, u * P : (u + 1) * P], ident[:]
            )
        mu_grouped = keep.tile([P, K, PACK], BF16, align_bytes=64)
        nc.vector.tensor_copy(
            out=mu_grouped[:].bitcast(F32), in_=mu_flipped[:].rearrange("p u k -> p k u")
        )
        empty_and_refill(2)
        empty_and_refill(3)
        quantise_by_feature(2)
        mu_codes = keep.tile([P, K], U32, align_bytes=64)
        mu_scales = keep.tile([P, K], U8, align_bytes=64)
        nc.vector.quantize_mx(
            out=mu_codes[:].bitcast(FP8X4),
            scales=mu_scales[:],
            in_=mu_grouped[:].rearrange("p k t -> p (k t)"),
        )
        for c in range(4, CHUNKS):
            empty_and_refill(c)
        for c in range(3, FEATURE_LEAD):
            quantise_by_feature(c)

        def store_mu():
            mu = keep.tile([P, D], F32, name="mu")
            nc.scalar.activation(out=mu[:], in_=mu_sum[:], func=ACT.Copy, scale=inv_colsum[:, 0:1])
            nc.sync.dma_start(out=out_0, in_=mu[:])

        logits = {}
        top = {}
        weights = {}
        total = {}
        shift = {}
        inv_total = {}

        def scores(c):
            logits[c] = banks.tile([P, PACK, K], F32, tag="bank", name="logits")
            for j in range(PACK):
                nc.tensor.matmul_mx(
                    out=logits[c][:, j, :],
                    lhsT=xf_codes[c][:, j * P : (j + 1) * P].bitcast(FP8X4),
                    lhsT_scale=xf_scales[c][:, j * P : (j + 1) * P],
                    rhs=mu_codes[:].bitcast(FP8X4),
                    rhs_scale=mu_scales[:],
                    start=True,
                    stop=True,
                )
            top[c] = small.tile([P, PACK], F32, name="top")
            nc.vector.tensor_reduce(out=top[c][:], in_=logits[c][:], axis=AXIS.X, op=ALU.max)

        def shift_rows(c):
            shift[c] = small.tile([P, PACK], F32, name="shift")
            nc.vector.tensor_scalar_mul(out=shift[c][:], in0=top[c][:], scalar1=-BETA)

        def exponentials(c):
            weights[c] = results.tile([P, PACK, K], F32, name="weights")
            total[c] = small.tile([P, PACK], F32, name="total")
            for j in range(PACK):
                nc.scalar.activation(
                    out=weights[c][:, j, :],
                    in_=logits[c][:, j, :],
                    func=ACT.Exp,
                    bias=shift[c][:, j : j + 1],
                    scale=BETA,
                    accum_out=total[c][:, j : j + 1],
                )

        def invert_totals(c):
            inv_total[c] = small.tile([P, PACK], F32, name="inv_total")
            if not (TAIL and c == CHUNKS - 1):
                nc.vector.reciprocal(inv_total[c][:], total[c][:])

        def divide_and_store(c):
            step = PACK // 2 if TAIL and c == CHUNKS - 1 else PACK
            for first in range(0, PACK, step):
                rows = slice(first, first + step)
                if step < PACK:
                    nc.vector.reciprocal(inv_total[c][:, rows], total[c][:, rows])
                for j in range(first, first + step):
                    if c in BY_SCALAR:
                        nc.scalar.activation(
                            out=weights[c][:, j, :],
                            in_=weights[c][:, j, :],
                            func=ACT.Copy,
                            scale=inv_total[c][:, j : j + 1],
                        )
                    else:
                        nc.vector.tensor_scalar_mul(
                            out=weights[c][:, j, :],
                            in0=weights[c][:, j, :],
                            scalar1=inv_total[c][:, j : j + 1],
                        )
                nc.sync.dma_start(out=r_new_chunks[c][:, rows, :], in_=weights[c][:, rows, :])

        for c in range(CHUNKS + DIVIDE_LAG):
            stage(scores, c)
            if QFIRST:
                stage(quantise_by_feature, c + FEATURE_LEAD)
            stage(invert_totals, c - DIVIDE_LAG)
            stage(shift_rows, c)
            if not QFIRST:
                stage(quantise_by_feature, c + FEATURE_LEAD)
            stage(divide_and_store, c - DIVIDE_LAG)
            stage(exponentials, c)
            if c == MU_AFTER:
                store_mu()
